import numpy as np
import ml_dtypes


def mxq(x, axis, fmt="e4m3"):
    dtype, down = {"e4m3": (ml_dtypes.float8_e4m3fn, 7), "e5m2": (ml_dtypes.float8_e5m2, 14)}[fmt]
    v = np.moveaxis(np.asarray(x, np.float32).astype(ml_dtypes.bfloat16).astype(np.float64), axis, -1)
    blocks = v.reshape(v.shape[:-1] + (-1, 32))
    amax = np.abs(blocks).max(-1, keepdims=True)
    byte = np.maximum(np.where(amax > 0, np.frexp(amax)[1] - 1 + 127, 0) - down, 1)
    scale = np.exp2(byte - 127.0)
    codes = (blocks / scale).astype(np.float32).astype(dtype).astype(np.float64)
    return np.moveaxis((codes * scale).reshape(v.shape), -1, axis)


WIDE = False


def mx_kscale(k):
    if not WIDE:
        return np.ones(k)
    levels = np.array([20, -20, 10, -10, 0])
    a = np.random.permutation(np.resize(levels, k // 512 * 4)).reshape(k // 512, 4)
    idx = np.arange(k)
    return np.exp2(a[idx // 512, idx % 128 // 32])


BF16 = ml_dtypes.bfloat16


def bf(x):
    return np.asarray(x, np.float32).astype(BF16)


def f64(x):
    return np.asarray(x).astype(np.float64)


B, J, I, O = 512, 8, 512, 128
IN_CH = J * I
OUT_CH = J * O
NEIGHBOUR_LIST = [[j for j in (i - 1, i, i + 1) if 0 <= j < J] for i in range(J)]


def build_mask():
    mask = np.zeros((OUT_CH, IN_CH))
    for i, neigh in enumerate(NEIGHBOUR_LIST):
        mask[i * O:(i + 1) * O, neigh[0] * I:(neigh[-1] + 1) * I] = 1.0
    return mask


def setup_inputs():
    s = mx_kscale(B)[:, None]
    keep = np.random.random((OUT_CH, IN_CH)) < 0.75
    x = np.random.standard_normal((B, IN_CH)) * s
    weight = np.random.standard_normal((OUT_CH, IN_CH)) / np.sqrt(0.75 * 3 * I)
    bias = np.random.standard_normal(OUT_CH) * 0.5
    g = np.random.standard_normal((B, OUT_CH)) * np.exp2(np.random.randint(-12, 1, (B, 1))) / s
    return {"x": bf(x),
            "weight": bf(weight),
            "mask": bf(build_mask() * keep),
            "bias": bf(bias),
            "grad_out": bf(g)}


def reference(x, weight, mask, bias, grad_out):
    x2 = f64(x).reshape(x.shape[0], -1)
    m = f64(mask)
    xq = mxq(x2, 0, "e4m3")
    gq = mxq(f64(grad_out), 0, "e5m2")
    out = np.zeros((OUT_CH, IN_CH))
    for i, neigh in enumerate(NEIGHBOUR_LIST):
        lo, hi = neigh[0] * I, (neigh[-1] + 1) * I
        r0, r1 = i * O, (i + 1) * O
        out[r0:r1, lo:hi] = (gq[:, r0:r1].T @ xq[:, lo:hi]) * m[r0:r1, lo:hi]
    return out

@@ -1,0 +1,119 @@
+from contextlib import ExitStack
+
+import concourse.mybir as mybir
+
+BF16 = mybir.dt.bfloat16
+F32 = mybir.dt.float32
+U32 = mybir.dt.uint32
+U8 = mybir.dt.uint8
+E4M3_X4 = mybir.dt.float8_e4m3fn_x4
+E5M2_X4 = mybir.dt.float8_e5m2_x4
+
+P = 128
+PACK = 4
+TOKENS = P * PACK
+JOINTS = 8
+IN_BLOCK = 512
+OUT_BLOCK = 128
+IN_CH = JOINTS * IN_BLOCK
+OUT_CH = JOINTS * OUT_BLOCK
+
+
+def neighbours(joint):
+    return range(max(joint - 1, 0), min(joint + 2, JOINTS))
+
+
+BLOCKS = 3 * JOINTS - 2
+FLOPS = 2 * BLOCKS * OUT_BLOCK * IN_BLOCK * TOKENS
+BYTES = 2 * (TOKENS * IN_CH + TOKENS * OUT_CH + BLOCKS * OUT_BLOCK * IN_BLOCK) + 4 * OUT_CH * IN_CH
+
+
+def tile_skeletonlinear_kernel(tc, x, weight, mask, bias, grad_out, out):
+    nc = tc.nc
+    assert tuple(x.shape) == (TOKENS, IN_CH)
+    assert tuple(grad_out.shape) == (TOKENS, OUT_CH)
+    assert tuple(mask.shape) == (OUT_CH, IN_CH)
+    assert tuple(out.shape) == (OUT_CH, IN_CH)
+
+    with ExitStack() as ctx:
+        keep = ctx.enter_context(tc.tile_pool(name="keep", bufs=1))
+        per_joint = ctx.enter_context(tc.tile_pool(name="per_joint", bufs=JOINTS))
+        psum = ctx.enter_context(tc.psum_pool(name="psum", bufs=4))
+
+        g_raw = keep.tile([P, PACK, OUT_CH], BF16)
+        nc.sync.dma_start(out=g_raw[:], in_=grad_out.rearrange("(p j) w -> p j w", j=PACK))
+        x_raw = keep.tile([P, PACK, IN_CH], BF16)
+        nc.sync.dma_start(out=x_raw[:], in_=x.rearrange("(p j) w -> p j w", j=PACK))
+
+        rows_of = [slice(joint * OUT_BLOCK, (joint + 1) * OUT_BLOCK) for joint in range(JOINTS)]
+        first_col = [neighbours(joint)[0] * IN_BLOCK for joint in range(JOINTS)]
+        end_col = [(neighbours(joint)[-1] + 1) * IN_BLOCK for joint in range(JOINTS)]
+        mask_tiles = []
+        for joint in range(JOINTS):
+            mask_sb = per_joint.tile([P, end_col[joint] - first_col[joint]], BF16)
+            nc.sync.dma_start(
+                out=mask_sb[:], in_=mask[rows_of[joint], first_col[joint] : end_col[joint]]
+            )
+            mask_tiles.append(mask_sb)
+
+        zeros = keep.tile([P, (JOINTS - 2) * IN_BLOCK], F32)
+        nc.vector.memset(zeros[:], 0.0)
+        for joint in range(JOINTS):
+            left = first_col[joint]
+            right = IN_CH - end_col[joint]
+            if left > 0:
+                nc.sync.dma_start(out=out[rows_of[joint], 0:left], in_=zeros[:, 0:left])
+            if right > 0:
+                nc.sync.dma_start(out=out[rows_of[joint], end_col[joint] : IN_CH], in_=zeros[:, 0:right])
+
+        g_grouped = keep.tile([P, OUT_CH, PACK], BF16, align_bytes=64)
+        g_codes = keep.tile([P, OUT_CH], U32, align_bytes=64)
+        g_scales = keep.tile([P, OUT_CH], U8, align_bytes=64)
+        nc.vector.tensor_copy(out=g_grouped[:], in_=g_raw[:].rearrange("p j w -> p w j"))
+        nc.vector.quantize_mx(
+            out=g_codes[:].bitcast(E5M2_X4),
+            scales=g_scales[:],
+            in_=g_grouped[:].rearrange("p w j -> p (w j)"),
+        )
+
+        x_grouped = keep.tile([P, IN_CH, PACK], BF16, align_bytes=64)
+        x_codes = keep.tile([P, IN_CH], U32, align_bytes=64)
+        x_scales = keep.tile([P, IN_CH], U8, align_bytes=64)
+        cols_of = [slice(joint * IN_BLOCK, (joint + 1) * IN_BLOCK) for joint in range(JOINTS)]
+        for joint in range(JOINTS):
+            regrouped = x_grouped[:, cols_of[joint], :]
+            as_loaded = x_raw[:, :, cols_of[joint]].rearrange("p j w -> p w j")
+            if joint % 2 == 0:
+                nc.vector.tensor_copy(out=regrouped, in_=as_loaded)
+            else:
+                nc.scalar.copy(out=regrouped, in_=as_loaded)
+        for joint in range(JOINTS):
+            nc.vector.quantize_mx(
+                out=x_codes[:, cols_of[joint]].bitcast(E4M3_X4),
+                scales=x_scales[:, cols_of[joint]],
+                in_=x_grouped[:, cols_of[joint], :].rearrange("p w j -> p (w j)"),
+            )
+
+        for joint in range(JOINTS):
+            product = per_joint.tile([P, end_col[joint] - first_col[joint]], F32)
+            for place, neighbour in enumerate(neighbours(joint)):
+                acc = psum.tile([OUT_BLOCK, IN_BLOCK], F32)
+                nc.tensor.matmul_mx(
+                    out=acc[:],
+                    lhsT=g_codes[:, rows_of[joint]].bitcast(E5M2_X4),
+                    lhsT_scale=g_scales[:, rows_of[joint]],
+                    rhs=x_codes[:, cols_of[neighbour]].bitcast(E4M3_X4),
+                    rhs_scale=x_scales[:, cols_of[neighbour]],
+                    start=True,
+                    stop=True,
+                )
+                here = slice(place * IN_BLOCK, (place + 1) * IN_BLOCK)
+                nc.vector.tensor_tensor(
+                    out=product[:, here],
+                    in0=acc[:],
+                    in1=mask_tiles[joint][:, here],
+                    op=mybir.AluOpType.mult,
+                )
+            nc.sync.dma_start(
+                out=out[rows_of[joint], first_col[joint] : end_col[joint]], in_=product[:]
+            )

@@ -17,15 +17,15 @@ IN_BLOCK = 512
 OUT_BLOCK = 128
 IN_CH = JOINTS * IN_BLOCK
 OUT_CH = JOINTS * OUT_BLOCK
-
-
-def neighbours(joint):
-    return range(max(joint - 1, 0), min(joint + 2, JOINTS))
-
+ENDS = (0, JOINTS - 1)
 
 BLOCKS = 3 * JOINTS - 2
 FLOPS = 2 * BLOCKS * OUT_BLOCK * IN_BLOCK * TOKENS
 BYTES = 2 * (TOKENS * IN_CH + TOKENS * OUT_CH + BLOCKS * OUT_BLOCK * IN_BLOCK) + 4 * OUT_CH * IN_CH
+
+
+def neighbours(joint):
+    return range(max(joint - 1, 0), min(joint + 2, JOINTS))
 
 
 def tile_skeletonlinear_kernel(tc, x, weight, mask, bias, grad_out, out):
@@ -35,19 +35,23 @@ def tile_skeletonlinear_kernel(tc, x, weight, mask, bias, grad_out, out):
     assert tuple(mask.shape) == (OUT_CH, IN_CH)
     assert tuple(out.shape) == (OUT_CH, IN_CH)
 
+    rows_of = [slice(joint * OUT_BLOCK, (joint + 1) * OUT_BLOCK) for joint in range(JOINTS)]
+    cols_of = [slice(joint * IN_BLOCK, (joint + 1) * IN_BLOCK) for joint in range(JOINTS)]
+    first_col = [neighbours(joint)[0] * IN_BLOCK for joint in range(JOINTS)]
+    end_col = [(neighbours(joint)[-1] + 1) * IN_BLOCK for joint in range(JOINTS)]
+
     with ExitStack() as ctx:
         keep = ctx.enter_context(tc.tile_pool(name="keep", bufs=1))
+        stage = ctx.enter_context(tc.tile_pool(name="stage", bufs=4))
         per_joint = ctx.enter_context(tc.tile_pool(name="per_joint", bufs=JOINTS))
+        per_end = ctx.enter_context(tc.tile_pool(name="per_end", bufs=len(ENDS)))
+        per_middle = ctx.enter_context(tc.tile_pool(name="per_middle", bufs=JOINTS - len(ENDS)))
         psum = ctx.enter_context(tc.psum_pool(name="psum", bufs=4))
 
         g_raw = keep.tile([P, PACK, OUT_CH], BF16)
         nc.sync.dma_start(out=g_raw[:], in_=grad_out.rearrange("(p j) w -> p j w", j=PACK))
         x_raw = keep.tile([P, PACK, IN_CH], BF16)
         nc.sync.dma_start(out=x_raw[:], in_=x.rearrange("(p j) w -> p j w", j=PACK))
-
-        rows_of = [slice(joint * OUT_BLOCK, (joint + 1) * OUT_BLOCK) for joint in range(JOINTS)]
-        first_col = [neighbours(joint)[0] * IN_BLOCK for joint in range(JOINTS)]
-        end_col = [(neighbours(joint)[-1] + 1) * IN_BLOCK for joint in range(JOINTS)]
         mask_tiles = []
         for joint in range(JOINTS):
             mask_sb = per_joint.tile([P, end_col[joint] - first_col[joint]], BF16)
@@ -58,13 +62,8 @@ def tile_skeletonlinear_kernel(tc, x, weight, mask, bias, grad_out, out):
 
         zeros = keep.tile([P, (JOINTS - 2) * IN_BLOCK], F32)
         nc.vector.memset(zeros[:], 0.0)
-        for joint in range(JOINTS):
-            left = first_col[joint]
-            right = IN_CH - end_col[joint]
-            if left > 0:
-                nc.sync.dma_start(out=out[rows_of[joint], 0:left], in_=zeros[:, 0:left])
-            if right > 0:
-                nc.sync.dma_start(out=out[rows_of[joint], end_col[joint] : IN_CH], in_=zeros[:, 0:right])
+        nc.sync.dma_start(out=out[rows_of[0], end_col[0] : IN_CH], in_=zeros[:])
+        nc.sync.dma_start(out=out[rows_of[JOINTS - 1], 0 : first_col[JOINTS - 1]], in_=zeros[:])
 
         g_grouped = keep.tile([P, OUT_CH, PACK], BF16, align_bytes=64)
         g_codes = keep.tile([P, OUT_CH], U32, align_bytes=64)
@@ -76,26 +75,42 @@ def tile_skeletonlinear_kernel(tc, x, weight, mask, bias, grad_out, out):
             in_=g_grouped[:].rearrange("p w j -> p (w j)"),
         )
 
-        x_grouped = keep.tile([P, IN_CH, PACK], BF16, align_bytes=64)
         x_codes = keep.tile([P, IN_CH], U32, align_bytes=64)
         x_scales = keep.tile([P, IN_CH], U8, align_bytes=64)
-        cols_of = [slice(joint * IN_BLOCK, (joint + 1) * IN_BLOCK) for joint in range(JOINTS)]
-        for joint in range(JOINTS):
-            regrouped = x_grouped[:, cols_of[joint], :]
-            as_loaded = x_raw[:, :, cols_of[joint]].rearrange("p j w -> p w j")
-            if joint % 2 == 0:
-                nc.vector.tensor_copy(out=regrouped, in_=as_loaded)
-            else:
-                nc.scalar.copy(out=regrouped, in_=as_loaded)
-        for joint in range(JOINTS):
+
+        def quantise_x(joint, x_grouped):
             nc.vector.quantize_mx(
                 out=x_codes[:, cols_of[joint]].bitcast(E4M3_X4),
                 scales=x_scales[:, cols_of[joint]],
-                in_=x_grouped[:, cols_of[joint], :].rearrange("p w j -> p (w j)"),
+                in_=x_grouped[:].rearrange("p w j -> p (w j)"),
             )
 
+        before = None
         for joint in range(JOINTS):
-            product = per_joint.tile([P, end_col[joint] - first_col[joint]], F32)
+            x_grouped = stage.tile([P, IN_BLOCK, PACK], BF16, align_bytes=64)
+            as_loaded = x_raw[:, :, cols_of[joint]].rearrange("p j w -> p w j")
+            if joint % 2 == 0:
+                nc.vector.tensor_copy(out=x_grouped[:], in_=as_loaded)
+            else:
+                nc.scalar.copy(out=x_grouped[:], in_=as_loaded)
+            if joint > 0:
+                quantise_x(joint - 1, before)
+            before = x_grouped
+        quantise_x(JOINTS - 1, before)
+
+        for joint in range(JOINTS):
+            if joint in ENDS:
+                result = per_end.tile([P, end_col[joint] - first_col[joint]], F32)
+                products = result[:]
+                target = out[rows_of[joint], first_col[joint] : end_col[joint]]
+            else:
+                result = per_middle.tile([P, IN_CH], F32)
+                if first_col[joint] > 0:
+                    nc.vector.memset(result[:, 0 : first_col[joint]], 0.0)
+                if end_col[joint] < IN_CH:
+                    nc.vector.memset(result[:, end_col[joint] : IN_CH], 0.0)
+                products = result[:, first_col[joint] : end_col[joint]]
+                target = out[rows_of[joint], :]
             for place, neighbour in enumerate(neighbours(joint)):
                 acc = psum.tile([OUT_BLOCK, IN_BLOCK], F32)
                 nc.tensor.matmul_mx(
@@ -109,11 +124,9 @@ def tile_skeletonlinear_kernel(tc, x, weight, mask, bias, grad_out, out):
                 )
                 here = slice(place * IN_BLOCK, (place + 1) * IN_BLOCK)
                 nc.vector.tensor_tensor(
-                    out=product[:, here],
+                    out=products[:, here],
                     in0=acc[:],
                     in1=mask_tiles[joint][:, here],
                     op=mybir.AluOpType.mult,
                 )
-            nc.sync.dma_start(
-                out=out[rows_of[joint], first_col[joint] : end_col[joint]], in_=product[:]
-            )
+            nc.sync.dma_start(out=target, in_=result[:])

@@ -78,6 +78,15 @@ def tile_skeletonlinear_kernel(tc, x, weight, mask, bias, grad_out, out):
         x_codes = keep.tile([P, IN_CH], U32, align_bytes=64)
         x_scales = keep.tile([P, IN_CH], U8, align_bytes=64)
 
+        def regroup_x(joint):
+            x_grouped = stage.tile([P, IN_BLOCK, PACK], BF16, align_bytes=64)
+            as_loaded = x_raw[:, :, cols_of[joint]].rearrange("p j w -> p w j")
+            if joint % 2 == 0:
+                nc.vector.tensor_copy(out=x_grouped[:], in_=as_loaded)
+            else:
+                nc.scalar.copy(out=x_grouped[:], in_=as_loaded)
+            return x_grouped
+
         def quantise_x(joint, x_grouped):
             nc.vector.quantize_mx(
                 out=x_codes[:, cols_of[joint]].bitcast(E4M3_X4),
@@ -85,30 +94,19 @@ def tile_skeletonlinear_kernel(tc, x, weight, mask, bias, grad_out, out):
                 in_=x_grouped[:].rearrange("p w j -> p (w j)"),
             )
 
-        before = None
-        for joint in range(JOINTS):
-            x_grouped = stage.tile([P, IN_BLOCK, PACK], BF16, align_bytes=64)
-            as_loaded = x_raw[:, :, cols_of[joint]].rearrange("p j w -> p w j")
-            if joint % 2 == 0:
-                nc.vector.tensor_copy(out=x_grouped[:], in_=as_loaded)
-            else:
-                nc.scalar.copy(out=x_grouped[:], in_=as_loaded)
-            if joint > 0:
-                quantise_x(joint - 1, before)
-            before = x_grouped
-        quantise_x(JOINTS - 1, before)
-
-        for joint in range(JOINTS):
+        def multiply_and_store(joint):
             if joint in ENDS:
                 result = per_end.tile([P, end_col[joint] - first_col[joint]], F32)
                 products = result[:]
                 target = out[rows_of[joint], first_col[joint] : end_col[joint]]
             else:
                 result = per_middle.tile([P, IN_CH], F32)
-                if first_col[joint] > 0:
-                    nc.vector.memset(result[:, 0 : first_col[joint]], 0.0)
-                if end_col[joint] < IN_CH:
-                    nc.vector.memset(result[:, end_col[joint] : IN_CH], 0.0)
+                left = first_col[joint]
+                right = IN_CH - end_col[joint]
+                if left > 0:
+                    nc.scalar.copy(out=result[:, 0:left], in_=zeros[:, 0:left])
+                if right > 0:
+                    nc.scalar.copy(out=result[:, end_col[joint] : IN_CH], in_=zeros[:, 0:right])
                 products = result[:, first_col[joint] : end_col[joint]]
                 target = out[rows_of[joint], :]
             for place, neighbour in enumerate(neighbours(joint)):
@@ -130,3 +128,13 @@ def tile_skeletonlinear_kernel(tc, x, weight, mask, bias, grad_out, out):
                     op=mybir.AluOpType.mult,
                 )
             nc.sync.dma_start(out=target, in_=result[:])
+
+        grouped_now = regroup_x(0)
+        for joint in range(JOINTS):
+            if joint + 1 < JOINTS:
+                grouped_next = regroup_x(joint + 1)
+            quantise_x(joint, grouped_now)
+            grouped_now = grouped_next
+            if joint > 0:
+                multiply_and_store(joint - 1)
+        multiply_and_store(JOINTS - 1)

@@ -18,6 +18,7 @@ OUT_BLOCK = 128
 IN_CH = JOINTS * IN_BLOCK
 OUT_CH = JOINTS * OUT_BLOCK
 ENDS = (0, JOINTS - 1)
+DMA_ALIGN = 256
 
 BLOCKS = 3 * JOINTS - 2
 FLOPS = 2 * BLOCKS * OUT_BLOCK * IN_BLOCK * TOKENS
@@ -48,19 +49,21 @@ def tile_skeletonlinear_kernel(tc, x, weight, mask, bias, grad_out, out):
         per_middle = ctx.enter_context(tc.tile_pool(name="per_middle", bufs=JOINTS - len(ENDS)))
         psum = ctx.enter_context(tc.psum_pool(name="psum", bufs=4))
 
-        g_raw = keep.tile([P, PACK, OUT_CH], BF16)
+        g_raw = keep.tile([P, PACK, OUT_CH], BF16, align_bytes=DMA_ALIGN)
         nc.sync.dma_start(out=g_raw[:], in_=grad_out.rearrange("(p j) w -> p j w", j=PACK))
-        x_raw = keep.tile([P, PACK, IN_CH], BF16)
+        x_raw = keep.tile([P, PACK, IN_CH], BF16, align_bytes=DMA_ALIGN)
         nc.sync.dma_start(out=x_raw[:], in_=x.rearrange("(p j) w -> p j w", j=PACK))
         mask_tiles = []
         for joint in range(JOINTS):
-            mask_sb = per_joint.tile([P, end_col[joint] - first_col[joint]], BF16)
+            mask_sb = per_joint.tile(
+                [P, end_col[joint] - first_col[joint]], BF16, align_bytes=DMA_ALIGN
+            )
             nc.sync.dma_start(
                 out=mask_sb[:], in_=mask[rows_of[joint], first_col[joint] : end_col[joint]]
             )
             mask_tiles.append(mask_sb)
 
-        zeros = keep.tile([P, (JOINTS - 2) * IN_BLOCK], F32)
+        zeros = keep.tile([P, (JOINTS - 2) * IN_BLOCK], F32, align_bytes=DMA_ALIGN)
         nc.vector.memset(zeros[:], 0.0)
         nc.sync.dma_start(out=out[rows_of[0], end_col[0] : IN_CH], in_=zeros[:])
         nc.sync.dma_start(out=out[rows_of[JOINTS - 1], 0 : first_col[JOINTS - 1]], in_=zeros[:])
@@ -96,11 +99,13 @@ def tile_skeletonlinear_kernel(tc, x, weight, mask, bias, grad_out, out):
 
         def multiply_and_store(joint):
             if joint in ENDS:
-                result = per_end.tile([P, end_col[joint] - first_col[joint]], F32)
+                result = per_end.tile(
+                    [P, end_col[joint] - first_col[joint]], F32, align_bytes=DMA_ALIGN
+                )
                 products = result[:]
                 target = out[rows_of[joint], first_col[joint] : end_col[joint]]
             else:
-                result = per_middle.tile([P, IN_CH], F32)
+                result = per_middle.tile([P, IN_CH], F32, align_bytes=DMA_ALIGN)
                 left = first_col[joint]
                 right = IN_CH - end_col[joint]
                 if left > 0:

@@ -18,7 +18,7 @@ OUT_BLOCK = 128
 IN_CH = JOINTS * IN_BLOCK
 OUT_CH = JOINTS * OUT_BLOCK
 ENDS = (0, JOINTS - 1)
-DMA_ALIGN = 256
+DMA_ALIGN = 1024
 
 BLOCKS = 3 * JOINTS - 2
 FLOPS = 2 * BLOCKS * OUT_BLOCK * IN_BLOCK * TOKENS

@@ -44,7 +44,7 @@ def tile_skeletonlinear_kernel(tc, x, weight, mask, bias, grad_out, out):
     with ExitStack() as ctx:
         keep = ctx.enter_context(tc.tile_pool(name="keep", bufs=1))
         stage = ctx.enter_context(tc.tile_pool(name="stage", bufs=4))
-        per_joint = ctx.enter_context(tc.tile_pool(name="per_joint", bufs=JOINTS))
+        per_triple = ctx.enter_context(tc.tile_pool(name="per_triple", bufs=2))
         per_end = ctx.enter_context(tc.tile_pool(name="per_end", bufs=len(ENDS)))
         per_middle = ctx.enter_context(tc.tile_pool(name="per_middle", bufs=JOINTS - len(ENDS)))
         psum = ctx.enter_context(tc.psum_pool(name="psum", bufs=4))
@@ -53,15 +53,33 @@ def tile_skeletonlinear_kernel(tc, x, weight, mask, bias, grad_out, out):
         nc.sync.dma_start(out=g_raw[:], in_=grad_out.rearrange("(p j) w -> p j w", j=PACK))
         x_raw = keep.tile([P, PACK, IN_CH], BF16, align_bytes=DMA_ALIGN)
         nc.sync.dma_start(out=x_raw[:], in_=x.rearrange("(p j) w -> p j w", j=PACK))
-        mask_tiles = []
-        for joint in range(JOINTS):
-            mask_sb = per_joint.tile(
-                [P, end_col[joint] - first_col[joint]], BF16, align_bytes=DMA_ALIGN
+        step = OUT_BLOCK * IN_CH + IN_BLOCK
+        window = 3 * IN_BLOCK
+        flat_mask = mask.rearrange("r c -> (r c)")
+
+        def load_mask_of_end(joint):
+            mask_sb = per_end.tile(
+                [P, end_col[joint] - first_col[joint]], BF16, align_bytes=DMA_ALIGN, name="mask_end"
             )
             nc.sync.dma_start(
                 out=mask_sb[:], in_=mask[rows_of[joint], first_col[joint] : end_col[joint]]
             )
-            mask_tiles.append(mask_sb)
+            return [mask_sb[:]]
+
+        def load_masks_of_three(joint):
+            start = joint * OUT_BLOCK * IN_CH + first_col[joint]
+            mask_sb = per_triple.tile([P, 3, window], BF16, align_bytes=DMA_ALIGN, name="mask_mid")
+            blocks = flat_mask[start : start + 3 * step].rearrange("(i q) -> i q", i=3)
+            blocks = blocks[:, 0 : OUT_BLOCK * IN_CH].rearrange("i (r c) -> r i c", c=IN_CH)
+            nc.sync.dma_start(out=mask_sb[:], in_=blocks[:, :, 0:window])
+            return [mask_sb[:, i, :] for i in range(3)]
+
+        mask_tiles = (
+            load_mask_of_end(0)
+            + load_masks_of_three(1)
+            + load_masks_of_three(4)
+            + load_mask_of_end(JOINTS - 1)
+        )
 
         zeros = keep.tile([P, (JOINTS - 2) * IN_BLOCK], F32, align_bytes=DMA_ALIGN)
         nc.vector.memset(zeros[:], 0.0)

@@ -20,6 +20,8 @@ OUT_CH = JOINTS * OUT_BLOCK
 ENDS = (0, JOINTS - 1)
 DMA_ALIGN = 1024
 
+LOWER_COLS = 128
+
 BLOCKS = 3 * JOINTS - 2
 FLOPS = 2 * BLOCKS * OUT_BLOCK * IN_BLOCK * TOKENS
 BYTES = 2 * (TOKENS * IN_CH + TOKENS * OUT_CH + BLOCKS * OUT_BLOCK * IN_BLOCK) + 4 * OUT_CH * IN_CH
@@ -44,7 +46,6 @@ def tile_skeletonlinear_kernel(tc, x, weight, mask, bias, grad_out, out):
     with ExitStack() as ctx:
         keep = ctx.enter_context(tc.tile_pool(name="keep", bufs=1))
         stage = ctx.enter_context(tc.tile_pool(name="stage", bufs=4))
-        per_triple = ctx.enter_context(tc.tile_pool(name="per_triple", bufs=2))
         per_end = ctx.enter_context(tc.tile_pool(name="per_end", bufs=len(ENDS)))
         per_middle = ctx.enter_context(tc.tile_pool(name="per_middle", bufs=JOINTS - len(ENDS)))
         psum = ctx.enter_context(tc.psum_pool(name="psum", bufs=4))
@@ -55,6 +56,7 @@ def tile_skeletonlinear_kernel(tc, x, weight, mask, bias, grad_out, out):
         nc.sync.dma_start(out=x_raw[:], in_=x.rearrange("(p j) w -> p j w", j=PACK))
         step = OUT_BLOCK * IN_CH + IN_BLOCK
         window = 3 * IN_BLOCK
+        middles = JOINTS - len(ENDS)
         flat_mask = mask.rearrange("r c -> (r c)")
 
         def load_mask_of_end(joint):
@@ -66,25 +68,31 @@ def tile_skeletonlinear_kernel(tc, x, weight, mask, bias, grad_out, out):
             )
             return [mask_sb[:]]
 
-        def load_masks_of_three(joint):
-            start = joint * OUT_BLOCK * IN_CH + first_col[joint]
-            mask_sb = per_triple.tile([P, 3, window], BF16, align_bytes=DMA_ALIGN, name="mask_mid")
-            blocks = flat_mask[start : start + 3 * step].rearrange("(i q) -> i q", i=3)
+        def load_masks_of_middle():
+            start = OUT_BLOCK * IN_CH + first_col[1]
+            mask_sb = keep.tile([P, middles, window], BF16, align_bytes=DMA_ALIGN, name="mask_mid")
+            blocks = flat_mask[start : start + middles * step].rearrange("(i q) -> i q", i=middles)
             blocks = blocks[:, 0 : OUT_BLOCK * IN_CH].rearrange("i (r c) -> r i c", c=IN_CH)
             nc.sync.dma_start(out=mask_sb[:], in_=blocks[:, :, 0:window])
-            return [mask_sb[:, i, :] for i in range(3)]
+            return [mask_sb[:, i, :] for i in range(middles)]
 
         mask_tiles = (
             load_mask_of_end(0)
-            + load_masks_of_three(1)
-            + load_masks_of_three(4)
+            + load_masks_of_middle()
             + load_mask_of_end(JOINTS - 1)
         )
 
         zeros = keep.tile([P, (JOINTS - 2) * IN_BLOCK], F32, align_bytes=DMA_ALIGN)
         nc.vector.memset(zeros[:], 0.0)
         nc.sync.dma_start(out=out[rows_of[0], end_col[0] : IN_CH], in_=zeros[:])
-        nc.sync.dma_start(out=out[rows_of[JOINTS - 1], 0 : first_col[JOINTS - 1]], in_=zeros[:])
+        last = rows_of[JOINTS - 1]
+        wide = first_col[JOINTS - 1] - LOWER_COLS
+        nc.sync.dma_start(out=out[last, 0:wide], in_=zeros[:, 0:wide])
+        rest = out[last, wide : first_col[JOINTS - 1]].rearrange("(a b) c -> a b c", a=8)
+        nc.sync.dma_start(
+            out=rest,
+            in_=zeros[0:32:4, 0 : P // 8 * LOWER_COLS].rearrange("a (b c) -> a b c", c=LOWER_COLS),
+        )
 
         g_grouped = keep.tile([P, OUT_CH, PACK], BF16, align_bytes=64)
         g_codes = keep.tile([P, OUT_CH], U32, align_bytes=64)

from contextlib import ExitStack

import concourse.mybir as mybir

BF16 = mybir.dt.bfloat16
F32 = mybir.dt.float32
U32 = mybir.dt.uint32
U8 = mybir.dt.uint8
E4M3_X4 = mybir.dt.float8_e4m3fn_x4
E5M2_X4 = mybir.dt.float8_e5m2_x4

P = 128
PACK = 4
TOKENS = P * PACK
JOINTS = 8
IN_BLOCK = 512
OUT_BLOCK = 128
IN_CH = JOINTS * IN_BLOCK
OUT_CH = JOINTS * OUT_BLOCK
ENDS = (0, JOINTS - 1)
DMA_ALIGN = 1024

LOWER_COLS = 128

BLOCKS = 3 * JOINTS - 2
FLOPS = 2 * BLOCKS * OUT_BLOCK * IN_BLOCK * TOKENS
BYTES = 2 * (TOKENS * IN_CH + TOKENS * OUT_CH + BLOCKS * OUT_BLOCK * IN_BLOCK) + 4 * OUT_CH * IN_CH


def neighbours(joint):
    return range(max(joint - 1, 0), min(joint + 2, JOINTS))


def tile_skeletonlinear_kernel(tc, x, weight, mask, bias, grad_out, out):
    nc = tc.nc
    assert tuple(x.shape) == (TOKENS, IN_CH)
    assert tuple(grad_out.shape) == (TOKENS, OUT_CH)
    assert tuple(mask.shape) == (OUT_CH, IN_CH)
    assert tuple(out.shape) == (OUT_CH, IN_CH)

    rows_of = [slice(joint * OUT_BLOCK, (joint + 1) * OUT_BLOCK) for joint in range(JOINTS)]
    cols_of = [slice(joint * IN_BLOCK, (joint + 1) * IN_BLOCK) for joint in range(JOINTS)]
    first_col = [neighbours(joint)[0] * IN_BLOCK for joint in range(JOINTS)]
    end_col = [(neighbours(joint)[-1] + 1) * IN_BLOCK for joint in range(JOINTS)]

    with ExitStack() as ctx:
        keep = ctx.enter_context(tc.tile_pool(name="keep", bufs=1))
        stage = ctx.enter_context(tc.tile_pool(name="stage", bufs=4))
        per_end = ctx.enter_context(tc.tile_pool(name="per_end", bufs=len(ENDS)))
        per_middle = ctx.enter_context(tc.tile_pool(name="per_middle", bufs=JOINTS - len(ENDS)))
        psum = ctx.enter_context(tc.psum_pool(name="psum", bufs=4))

        g_raw = keep.tile([P, PACK, OUT_CH], BF16, align_bytes=DMA_ALIGN)
        nc.sync.dma_start(out=g_raw[:], in_=grad_out.rearrange("(p j) w -> p j w", j=PACK))
        x_raw = keep.tile([P, PACK, IN_CH], BF16, align_bytes=DMA_ALIGN)
        nc.sync.dma_start(out=x_raw[:], in_=x.rearrange("(p j) w -> p j w", j=PACK))
        step = OUT_BLOCK * IN_CH + IN_BLOCK
        window = 3 * IN_BLOCK
        middles = JOINTS - len(ENDS)
        flat_mask = mask.rearrange("r c -> (r c)")

        def load_mask_of_end(joint):
            mask_sb = per_end.tile(
                [P, end_col[joint] - first_col[joint]], BF16, align_bytes=DMA_ALIGN, name="mask_end"
            )
            nc.sync.dma_start(
                out=mask_sb[:], in_=mask[rows_of[joint], first_col[joint] : end_col[joint]]
            )
            return [mask_sb[:]]

        def load_masks_of_middle():
            start = OUT_BLOCK * IN_CH + first_col[1]
            mask_sb = keep.tile([P, middles, window], BF16, align_bytes=DMA_ALIGN, name="mask_mid")
            blocks = flat_mask[start : start + middles * step].rearrange("(i q) -> i q", i=middles)
            blocks = blocks[:, 0 : OUT_BLOCK * IN_CH].rearrange("i (r c) -> r i c", c=IN_CH)
            nc.sync.dma_start(out=mask_sb[:], in_=blocks[:, :, 0:window])
            return [mask_sb[:, i, :] for i in range(middles)]

        mask_tiles = (
            load_mask_of_end(0)
            + load_masks_of_middle()
            + load_mask_of_end(JOINTS - 1)
        )

        zeros = keep.tile([P, (JOINTS - 2) * IN_BLOCK], F32, align_bytes=DMA_ALIGN)
        nc.vector.memset(zeros[:], 0.0)
        nc.sync.dma_start(out=out[rows_of[0], end_col[0] : IN_CH], in_=zeros[:])
        last = rows_of[JOINTS - 1]
        wide = first_col[JOINTS - 1] - LOWER_COLS
        nc.sync.dma_start(out=out[last, 0:wide], in_=zeros[:, 0:wide])
        rest = out[last, wide : first_col[JOINTS - 1]].rearrange("(a b) c -> a b c", a=8)
        nc.sync.dma_start(
            out=rest,
            in_=zeros[0:32:4, 0 : P // 8 * LOWER_COLS].rearrange("a (b c) -> a b c", c=LOWER_COLS),
        )

        g_grouped = keep.tile([P, OUT_CH, PACK], BF16, align_bytes=64)
        g_codes = keep.tile([P, OUT_CH], U32, align_bytes=64)
        g_scales = keep.tile([P, OUT_CH], U8, align_bytes=64)
        nc.vector.tensor_copy(out=g_grouped[:], in_=g_raw[:].rearrange("p j w -> p w j"))
        nc.vector.quantize_mx(
            out=g_codes[:].bitcast(E5M2_X4),
            scales=g_scales[:],
            in_=g_grouped[:].rearrange("p w j -> p (w j)"),
        )

        x_codes = keep.tile([P, IN_CH], U32, align_bytes=64)
        x_scales = keep.tile([P, IN_CH], U8, align_bytes=64)

        def regroup_x(joint):
            x_grouped = stage.tile([P, IN_BLOCK, PACK], BF16, align_bytes=64)
            as_loaded = x_raw[:, :, cols_of[joint]].rearrange("p j w -> p w j")
            if joint % 2 == 0:
                nc.vector.tensor_copy(out=x_grouped[:], in_=as_loaded)
            else:
                nc.scalar.copy(out=x_grouped[:], in_=as_loaded)
            return x_grouped

        def quantise_x(joint, x_grouped):
            nc.vector.quantize_mx(
                out=x_codes[:, cols_of[joint]].bitcast(E4M3_X4),
                scales=x_scales[:, cols_of[joint]],
                in_=x_grouped[:].rearrange("p w j -> p (w j)"),
            )

        def multiply_and_store(joint):
            if joint in ENDS:
                result = per_end.tile(
                    [P, end_col[joint] - first_col[joint]], F32, align_bytes=DMA_ALIGN
                )
                products = result[:]
                target = out[rows_of[joint], first_col[joint] : end_col[joint]]
            else:
                result = per_middle.tile([P, IN_CH], F32, align_bytes=DMA_ALIGN)
                left = first_col[joint]
                right = IN_CH - end_col[joint]
                if left > 0:
                    nc.scalar.copy(out=result[:, 0:left], in_=zeros[:, 0:left])
                if right > 0:
                    nc.scalar.copy(out=result[:, end_col[joint] : IN_CH], in_=zeros[:, 0:right])
                products = result[:, first_col[joint] : end_col[joint]]
                target = out[rows_of[joint], :]
            for place, neighbour in enumerate(neighbours(joint)):
                acc = psum.tile([OUT_BLOCK, IN_BLOCK], F32)
                nc.tensor.matmul_mx(
                    out=acc[:],
                    lhsT=g_codes[:, rows_of[joint]].bitcast(E5M2_X4),
                    lhsT_scale=g_scales[:, rows_of[joint]],
                    rhs=x_codes[:, cols_of[neighbour]].bitcast(E4M3_X4),
                    rhs_scale=x_scales[:, cols_of[neighbour]],
                    start=True,
                    stop=True,
                )
                here = slice(place * IN_BLOCK, (place + 1) * IN_BLOCK)
                nc.vector.tensor_tensor(
                    out=products[:, here],
                    in0=acc[:],
                    in1=mask_tiles[joint][:, here],
                    op=mybir.AluOpType.mult,
                )
            nc.sync.dma_start(out=target, in_=result[:])

        grouped_now = regroup_x(0)
        for joint in range(JOINTS):
            if joint + 1 < JOINTS:
                grouped_next = regroup_x(joint + 1)
            quantise_x(joint, grouped_now)
            grouped_now = grouped_next
            if joint > 0:
                multiply_and_store(joint - 1)
        multiply_and_store(JOINTS - 1)
